import numpy as np
import ml_dtypes


def mxq(x, axis, fmt="e4m3"):
    dtype, down = {"e4m3": (ml_dtypes.float8_e4m3fn, 7), "e5m2": (ml_dtypes.float8_e5m2, 14)}[fmt]
    v = np.moveaxis(np.asarray(x, np.float32).astype(ml_dtypes.bfloat16).astype(np.float64), axis, -1)
    blocks = v.reshape(v.shape[:-1] + (-1, 32))
    amax = np.abs(blocks).max(-1, keepdims=True)
    byte = np.maximum(np.where(amax > 0, np.frexp(amax)[1] - 1 + 127, 0) - down, 1)
    scale = np.exp2(byte - 127.0)
    codes = (blocks / scale).astype(np.float32).astype(dtype).astype(np.float64)
    return np.moveaxis((codes * scale).reshape(v.shape), -1, axis)


WIDE = False


def mx_kscale(k):
    if not WIDE:
        return np.ones(k)
    levels = np.array([10, -10, 5, -5, 0])
    a = np.random.permutation(np.resize(levels, k // 512 * 4)).reshape(k // 512, 4)
    idx = np.arange(k)
    return np.exp2(a[idx // 512, idx % 128 // 32])


BF16 = ml_dtypes.bfloat16


def bf(x):
    return np.asarray(x, np.float32).astype(BF16)


def f64(x):
    return np.asarray(x).astype(np.float64)


B, GH, GW, E, H, DH = 256, 7, 7, 512, 4, 32
S = GH * GW
N = H * DH
BASE = 100.0


def rope_half(xh, ang):
    x1, x2 = xh[..., 0::2], xh[..., 1::2]
    cos = np.cos(ang)[None, :, None, :]
    sin = np.sin(ang)[None, :, None, :]
    o1 = x1 * cos - x2 * sin
    o2 = x1 * sin + x2 * cos
    return np.stack([o1, o2], axis=-1).reshape(xh.shape)


def rope_2d(t):
    dh = DH // 2
    rows = f64(np.repeat(np.arange(GH), GW))
    cols = f64(np.tile(np.arange(GW), GH))
    inv_freq = BASE ** (-f64(np.arange(0, dh, 2)) / dh)
    ang_r = rows[:, None] * inv_freq[None, :]
    ang_c = cols[:, None] * inv_freq[None, :]
    tr = rope_half(t[..., :dh], ang_r)
    tc = rope_half(t[..., dh:], ang_c)
    return np.concatenate([tr, tc], axis=-1)


def setup_inputs():
    s = mx_kscale(E)
    w = 1.0 / np.sqrt(E)
    return {"x": bf(np.random.standard_normal((B, S, E)) * s),
            "Wq": bf(np.random.standard_normal((E, N)) * w / s[:, None]),
            "bq": bf(np.random.standard_normal(N) * 0.3),
            "Wk": bf(np.random.standard_normal((E, N)) * w / s[:, None]),
            "bk": bf(np.random.standard_normal(N) * 0.3)}


def reference(x, Wq, bq, Wk, bk):
    xq = mxq(f64(x), 2, "e4m3")
    q = ((xq @ mxq(f64(Wq), 0, "e4m3")) + f64(bq)).reshape(B, S, H, DH)
    k = ((xq @ mxq(f64(Wk), 0, "e4m3")) + f64(bk)).reshape(B, S, H, DH)
    return rope_2d(q), rope_2d(k)

@@ -1,0 +1,297 @@
+from contextlib import ExitStack
+
+import concourse.bass as bass
+import concourse.mybir as mybir
+import concourse.tile as tile
+from concourse.masks import make_identity
+
+F32 = mybir.dt.float32
+BF16 = mybir.dt.bfloat16
+U32 = mybir.dt.uint32
+U8 = mybir.dt.uint8
+FP8X4 = mybir.dt.float8_e4m3fn_x4
+ALU = mybir.AluOpType
+ACT = mybir.ActivationFunctionType
+
+P = 128
+IMAGES = 256
+GRID = 7
+NPOS = GRID * GRID
+E = 512
+WORDS = E // 2
+NF = 128
+BASE = 100.0
+FLOPS = 2 * IMAGES * NPOS * E * 2 * NF
+
+X_CHUNKS = [2, 4, 6, 8, 8, 8, 8, 5]
+O_CHUNKS = [8, 8, 8, 8, 8, 4, 2, 2, 1]
+SCALAR_EVAC_EVERY = 4
+
+
+def cos_sin(theta):
+    c, s, term = 0.0, 0.0, 1.0
+    for n in range(0, 30, 2):
+        c += term
+        term = term * theta / (n + 1)
+        s += term
+        term = -term * theta / (n + 2)
+    return c, s
+
+
+def chunk_table(lens):
+    table = []
+    for c, n in enumerate(lens):
+        for i in range(n):
+            table.append((c, i))
+    return table
+
+
+def tile_attention_pa_t_kernel(tc, x, Wq, bq, Wk, bk, out_0, out_1):
+    nc = tc.nc
+    assert sum(X_CHUNKS) == NPOS and sum(O_CHUNKS) == NPOS
+    x_of = chunk_table(X_CHUNKS)
+    o_of = chunk_table(O_CHUNKS)
+    xv = x.rearrange("(p h) s k -> p h s k", h=2)
+    ov = [o.rearrange("(p h) s a d -> p h s (a d)", h=2) for o in (out_0, out_1)]
+    nslot = (NPOS + 1) // 2
+
+    with ExitStack() as ctx:
+        ctx.enter_context(tc.manual_schedule())
+        const = ctx.enter_context(tc.tile_pool(name="const", bufs=1))
+        xpool = ctx.enter_context(tc.tile_pool(name="xpool", bufs=1))
+        work = ctx.enter_context(tc.tile_pool(name="work", bufs=2))
+        opool = ctx.enter_context(tc.tile_pool(name="opool", bufs=3))
+        ps_x = ctx.enter_context(tc.psum_pool(name="ps_x", bufs=1))
+        ps_p = ctx.enter_context(tc.psum_pool(name="ps_p", bufs=2))
+        ps_o = ctx.enter_context(tc.psum_pool(name="ps_o", bufs=1))
+
+        wraw = const.tile([P, 2, 4, NF], BF16, name="wraw")
+        for q, w in enumerate((Wq, Wk)):
+            nc.scalar.dma_start(
+                out=wraw[:, q, :, :].rearrange("p (u e) f -> p u (e f)", u=2),
+                in_=w.rearrange("(u p e) f -> p u (e f)", u=2, e=2),
+            )
+        xs = []
+        s0 = 0
+        for c, n in enumerate(X_CHUNKS):
+            xt_sb = xpool.tile([P, 2 * n * E], BF16, name="xs%d" % c)
+            nc.sync.dma_start(
+                out=xt_sb[:].rearrange("p (h s k) -> p h s k", h=2, s=n),
+                in_=xv[:, :, s0 : s0 + n, :],
+            )
+            xs.append(xt_sb)
+            s0 += n
+
+        ident = const.tile([P, P], F32, name="ident")
+        make_identity(nc, ident[:])
+        warm = const.tile([P, 2], F32, name="warm")
+        nc.gpsimd.memset(warm[:, 0:1], 0.0)
+        nc.scalar.activation(out=warm[:, 1:2], in_=warm[:, 0:1], func=ACT.Identity)
+
+        rw = const.tile([P, 3, P], F32, name="rw")
+        nc.vector.memset(rw[:], 0.0)
+        bst = const.tile([P, 2 * NF], BF16, name="bst")
+        nc.vector.memset(bst[:], 0.0)
+        nc.scalar.dma_start(out=bst[0:1, 0:NF], in_=bq.unsqueeze(0))
+        nc.scalar.dma_start(out=bst[0:1, NF : 2 * NF], in_=bk.unsqueeze(0))
+        for j in range(8):
+            theta = BASE ** (-(2.0 * j) / 16.0)
+            for v, val in enumerate(cos_sin(theta)):
+                col = rw[:, v, :].rearrange("p (g j) -> p g j", j=8)[:, :, j]
+                nc.vector.tensor_scalar(out=col, in0=col, scalar1=val, scalar2=None, op0=ALU.add)
+        nc.vector.memset(rw[:, 2, :].rearrange("p (g h j) -> p g h j", h=2, j=8)[:, :, 1, :], 1.0)
+
+        pt = ps_o.tile([P, 512], F32, name="pt", tag="ot0")
+        for v in range(3):
+            nc.tensor.transpose(pt[:, v * P : (v + 1) * P], rw[:, v, :], ident[:])
+
+        wg = const.tile([P, 2, P, 4], BF16, name="wg", align_bytes=64)
+        for ab in range(2):
+            nc.scalar.copy(
+                out=wg[:, ab, :, :].rearrange("p (q r) t -> p q r t", q=2),
+                in_=wraw[:].rearrange("p q t (r b) -> p b q r t", b=2)[:, ab],
+            )
+        wc = const.tile([P, 2 * P], U32, name="wc", align_bytes=64)
+        ws = const.tile([P, 2 * P], U8, name="ws", align_bytes=64)
+
+        tcs = const.tile([P, 2, GRID], F32, name="tcs")
+        h01 = const.tile([P, 2], F32, name="h01")
+        nc.vector.memset(tcs[:, 0, 0:1], 1.0)
+        nc.vector.memset(tcs[:, 1, 0:1], 0.0)
+        ptv = pt[:].rearrange("p (v n) -> p v n", n=P)
+        nc.vector.tensor_copy(out=tcs[:, :, 1], in_=ptv[:, 0:2, 0])
+        nc.vector.tensor_copy(out=h01[:, 1:2], in_=ptv[:, 2, 0:1])
+        nc.vector.tensor_scalar(out=h01[:, 0:1], in0=h01[:, 1:2], scalar1=-1.0, scalar2=1.0,
+                                op0=ALU.mult, op1=ALU.add)
+
+        def add_angle(k, lo, hi):
+            ck = tcs[:, 0, k : k + 1]
+            sk = tcs[:, 1, k : k + 1]
+            n = hi - lo
+            u = const.tile([P, 2, 2], F32, name="u%d" % k)
+            nc.vector.tensor_scalar(out=u[:, :, 0:n], in0=tcs[:, :, lo:hi], scalar1=sk, scalar2=None,
+                                    op0=ALU.mult)
+            nc.vector.scalar_tensor_tensor(out=tcs[:, 0, lo + k : hi + k], in0=tcs[:, 0, lo:hi], scalar=ck,
+                                           in1=u[:, 1, 0:n], op0=ALU.mult, op1=ALU.subtract)
+            nc.vector.scalar_tensor_tensor(out=tcs[:, 1, lo + k : hi + k], in0=tcs[:, 1, lo:hi], scalar=ck,
+                                           in1=u[:, 0, 0:n], op0=ALU.mult, op1=ALU.add)
+
+        add_angle(1, 1, 2)
+        add_angle(2, 1, 3)
+        add_angle(4, 1, 3)
+
+        cos_t = const.tile([P, NPOS], F32, name="cos_t")
+        sin_t = const.tile([P, NPOS], F32, name="sin_t")
+        nsin_t = const.tile([P, NPOS], F32, name="nsin_t")
+        bias_a = const.tile([P, NPOS], F32, name="bias_a")
+        bias_b = const.tile([P, NPOS], F32, name="bias_b")
+        tmp0 = const.tile([P, NPOS], F32, name="tmp0")
+        tmp1 = const.tile([P, NPOS], F32, name="tmp1")
+        for v, (dst, tmp) in enumerate(((cos_t, tmp0), (sin_t, tmp1))):
+            by_col = tcs[:, v, :].unsqueeze(1).to_broadcast([P, GRID, GRID])
+            by_row = tcs[:, v, :].unsqueeze(2).to_broadcast([P, GRID, GRID])
+            tv = tmp[:].rearrange("p (r c) -> p r c", c=GRID)
+            nc.vector.tensor_scalar(out=tv, in0=by_col, scalar1=h01[:, 1:2], scalar2=None, op0=ALU.mult)
+            nc.vector.scalar_tensor_tensor(out=dst[:].rearrange("p (r c) -> p r c", c=GRID), in0=by_row,
+                                           scalar=h01[:, 0:1], in1=tv, op0=ALU.mult, op1=ALU.add)
+        nc.vector.tensor_scalar(out=nsin_t[:], in0=sin_t[:], scalar1=-1.0, scalar2=None, op0=ALU.mult)
+
+        nc.vector.quantize_mx(out=wc[:].bitcast(FP8X4), scales=ws[:],
+                              in_=wg[:].rearrange("p b m t -> p (b m t)"))
+
+        rwb = const.tile([P, 2, P], F32, name="rwb")
+        nc.vector.tensor_copy(out=rwb[:], in_=bst[:].rearrange("p (m b) -> p b m", b=2))
+        pt2 = ps_o.tile([P, 512], F32, name="pt2", tag="ot1")
+        bab = const.tile([P, 2], F32, name="bab")
+        tmp2 = const.tile([P, NPOS], F32, name="tmp2")
+        tmp3 = const.tile([P, NPOS], F32, name="tmp3")
+
+        def bias_transposes():
+            for v in range(2):
+                nc.tensor.transpose(pt2[:, v * P : (v + 1) * P], rwb[:, v, :], ident[:])
+
+        def bias_tables():
+            nc.vector.tensor_copy(out=bab[:], in_=pt2[:].rearrange("p (v n) -> p v n", n=P)[:, 0:2, 0])
+            nc.vector.tensor_scalar(out=tmp2[:], in0=sin_t[:], scalar1=bab[:, 1:2], scalar2=None, op0=ALU.mult)
+            nc.vector.scalar_tensor_tensor(out=bias_a[:], in0=cos_t[:], scalar=bab[:, 0:1], in1=tmp2[:],
+                                           op0=ALU.mult, op1=ALU.subtract)
+            nc.vector.tensor_scalar(out=tmp3[:], in0=cos_t[:], scalar1=bab[:, 1:2], scalar2=None, op0=ALU.mult)
+            nc.vector.scalar_tensor_tensor(out=bias_b[:], in0=sin_t[:], scalar=bab[:, 0:1], in1=tmp3[:],
+                                           op0=ALU.mult, op1=ALU.add)
+
+        st = {}
+
+        def positions(n):
+            return [s for s in (2 * n, 2 * n + 1) if s < NPOS]
+
+        def stage_l(n):
+            for j, s in enumerate(positions(n)):
+                c, i = x_of[s]
+                x32 = xs[c][:].bitcast(F32)
+                xt = ps_x.tile([P, 512], F32, name="xt", tag="xt%d" % j)
+                for h in range(2):
+                    for u in range(2):
+                        off = (h * X_CHUNKS[c] + i) * WORDS + u * P
+                        nc.tensor.transpose(xt[:, (2 * h + u) * P : (2 * h + u + 1) * P],
+                                            x32[:, off : off + P], ident[:])
+                st["xt", s] = xt
+
+        def stage_e(n):
+            pos = positions(n)
+            xg = work.tile([P, 2048], BF16, name="xg", align_bytes=64)
+            st["xg", n] = xg
+            for j, s in enumerate(pos):
+                dst = xg[:, j * 1024 : (j + 1) * 1024].bitcast(F32).rearrange("p (h i u) -> p h i u", h=2, u=2)
+                src = st["xt", s][:].rearrange("p (h u i) -> p h i u", h=2, u=2)
+                if s % SCALAR_EVAC_EVERY == 1:
+                    nc.scalar.copy(out=dst, in_=src)
+                else:
+                    nc.vector.tensor_copy(out=dst, in_=src)
+
+        def stage_q(n):
+            w = 256 * len(positions(n))
+            xc = work.tile([P, 512], U32, name="xc", align_bytes=64)
+            xsc = work.tile([P, 512], U8, name="xsc", align_bytes=64)
+            nc.vector.quantize_mx(out=xc[:, 0:w].bitcast(FP8X4), scales=xsc[:, 0:w], in_=st["xg", n][:, 0 : 4 * w])
+            st["xc", n] = (xc, xsc)
+
+        def stage_m(n):
+            xc, xsc = st["xc", n]
+            for j, s in enumerate(positions(n)):
+                pp = ps_p.tile([P, 512], F32, name="pp", tag="pp%d" % j)
+                for ab in range(2):
+                    nc.tensor.matmul_mx(
+                        out=pp[:, ab * 256 : (ab + 1) * 256],
+                        lhsT=wc[:, ab * P : (ab + 1) * P].bitcast(FP8X4),
+                        lhsT_scale=ws[:, ab * P : (ab + 1) * P],
+                        rhs=xc[:, j * 256 : (j + 1) * 256].bitcast(FP8X4),
+                        rhs_scale=xsc[:, j * 256 : (j + 1) * 256],
+                        start=True,
+                        stop=True,
+                    )
+                st["pp", s] = pp
+
+        def stage_a(n):
+            for j, s in enumerate(positions(n)):
+                pp = st["pp", s]
+                tt = work.tile([P, 512], F32, name="tt", tag="tt%d" % j)
+                nc.scalar.activation(out=tt[:, 256:512], in_=pp[:, 256:512], func=ACT.Identity,
+                                     bias=bias_b[:, s : s + 1], scale=cos_t[:, s : s + 1])
+                nc.scalar.activation(out=tt[:, 0:256], in_=pp[:, 0:256], func=ACT.Identity,
+                                     bias=bias_a[:, s : s + 1], scale=cos_t[:, s : s + 1])
+                st["tt", s] = tt
+
+        def stage_b(n):
+            for j, s in enumerate(positions(n)):
+                pp = st["pp", s]
+                tt = st["tt", s]
+                oo = work.tile([P, 512], F32, name="oo", tag="oo%d" % j)
+                nc.vector.scalar_tensor_tensor(out=oo[:, 0:256], in0=pp[:, 256:512], scalar=nsin_t[:, s : s + 1],
+                                               in1=tt[:, 0:256], op0=ALU.mult, op1=ALU.add)
+                nc.vector.scalar_tensor_tensor(out=oo[:, 256:512], in0=pp[:, 0:256], scalar=sin_t[:, s : s + 1],
+                                               in1=tt[:, 256:512], op0=ALU.mult, op1=ALU.add)
+                st["oo", s] = oo
+
+        def stage_t(n):
+            for j, s in enumerate(positions(n)):
+                oo = st["oo", s]
+                ot = ps_o.tile([P, 512], F32, name="ot", tag="ot%d" % j)
+                for g in range(4):
+                    nc.tensor.transpose(ot[:, g * P : (g + 1) * P], oo[:, g * P : (g + 1) * P], ident[:])
+                st["ot", s] = ot
+
+        def stage_c(n):
+            for s in positions(n):
+                c, i = o_of[s]
+                ln = O_CHUNKS[c]
+                if i == 0:
+                    st["ob", c] = [opool.tile([P, 2 * 8 * NF], F32, name="ob%d" % q) for q in range(2)]
+                src = st["ot", s][:].rearrange("p (b h q m) -> p q h m b", b=2, h=2, q=2)
+                for q in range(2):
+                    dst = st["ob", c][q][:, 0 : 2 * ln * NF].rearrange("p (h s m b) -> p h s m b", h=2, s=ln, b=2)
+                    nc.scalar.copy(out=dst[:, :, i, :, :], in_=src[:, q])
+                if i == ln - 1:
+                    first = s - i
+                    for q in range(2):
+                        nc.sync.dma_start(
+                            out=ov[q][:, :, first : first + ln, :],
+                            in_=st["ob", c][q][:, 0 : 2 * ln * NF].rearrange("p (h s f) -> p h s f", h=2, s=ln),
+                        )
+
+        def run(stage, n):
+            if 0 <= n < nslot:
+                stage(n)
+
+        for t in range(-1, nslot + 2):
+            run(stage_l, t + 1)
+            if t == -1:
+                bias_transposes()
+            run(stage_q, t)
+            if t == 0:
+                bias_tables()
+            run(stage_a, t - 1)
+            run(stage_e, t + 1)
+            run(stage_t, t - 2)
+            run(stage_b, t - 1)
+            run(stage_c, t - 2)
+            run(stage_m, t)

@@ -65,6 +65,9 @@ def tile_attention_pa_t_kernel(tc, x, Wq, bq, Wk, bk, out_0, out_1):
         ps_p = ctx.enter_context(tc.psum_pool(name="ps_p", bufs=2))
         ps_o = ctx.enter_context(tc.psum_pool(name="ps_o", bufs=1))
 
+        bsm = const.tile([P, 2 * NF], BF16, name="bsm")
+        nc.scalar.dma_start(out=bsm[0:1, 0:NF], in_=bq.unsqueeze(0))
+        nc.scalar.dma_start(out=bsm[0:1, NF : 2 * NF], in_=bk.unsqueeze(0))
         wraw = const.tile([P, 2, 4, NF], BF16, name="wraw")
         for q, w in enumerate((Wq, Wk)):
             nc.scalar.dma_start(
@@ -90,10 +93,8 @@ def tile_attention_pa_t_kernel(tc, x, Wq, bq, Wk, bk, out_0, out_1):
 
         rw = const.tile([P, 3, P], F32, name="rw")
         nc.vector.memset(rw[:], 0.0)
-        bst = const.tile([P, 2 * NF], BF16, name="bst")
-        nc.vector.memset(bst[:], 0.0)
-        nc.scalar.dma_start(out=bst[0:1, 0:NF], in_=bq.unsqueeze(0))
-        nc.scalar.dma_start(out=bst[0:1, NF : 2 * NF], in_=bk.unsqueeze(0))
+        rwb = const.tile([P, 2, P], F32, name="rwb")
+        nc.vector.memset(rwb[:], 0.0)
         for j in range(8):
             theta = BASE ** (-(2.0 * j) / 16.0)
             for v, val in enumerate(cos_sin(theta)):
@@ -107,9 +108,10 @@ def tile_attention_pa_t_kernel(tc, x, Wq, bq, Wk, bk, out_0, out_1):
 
         wg = const.tile([P, 2, P, 4], BF16, name="wg", align_bytes=64)
         for ab in range(2):
-            nc.scalar.copy(
+            nc.scalar.mul(
                 out=wg[:, ab, :, :].rearrange("p (q r) t -> p q r t", q=2),
                 in_=wraw[:].rearrange("p q t (r b) -> p b q r t", b=2)[:, ab],
+                mul=(1.0, -1.0)[ab],
             )
         wc = const.tile([P, 2 * P], U32, name="wc", align_bytes=64)
         ws = const.tile([P, 2 * P], U8, name="ws", align_bytes=64)
@@ -142,7 +144,7 @@ def tile_attention_pa_t_kernel(tc, x, Wq, bq, Wk, bk, out_0, out_1):
 
         cos_t = const.tile([P, NPOS], F32, name="cos_t")
         sin_t = const.tile([P, NPOS], F32, name="sin_t")
-        nsin_t = const.tile([P, NPOS], F32, name="nsin_t")
+        ncos_t = const.tile([P, NPOS], F32, name="ncos_t")
         bias_a = const.tile([P, NPOS], F32, name="bias_a")
         bias_b = const.tile([P, NPOS], F32, name="bias_b")
         tmp0 = const.tile([P, NPOS], F32, name="tmp0")
@@ -154,21 +156,19 @@ def tile_attention_pa_t_kernel(tc, x, Wq, bq, Wk, bk, out_0, out_1):
             nc.vector.tensor_scalar(out=tv, in0=by_col, scalar1=h01[:, 1:2], scalar2=None, op0=ALU.mult)
             nc.vector.scalar_tensor_tensor(out=dst[:].rearrange("p (r c) -> p r c", c=GRID), in0=by_row,
                                            scalar=h01[:, 0:1], in1=tv, op0=ALU.mult, op1=ALU.add)
-        nc.vector.tensor_scalar(out=nsin_t[:], in0=sin_t[:], scalar1=-1.0, scalar2=None, op0=ALU.mult)
+        nc.vector.tensor_scalar(out=ncos_t[:], in0=cos_t[:], scalar1=-1.0, scalar2=None, op0=ALU.mult)
+        nc.vector.tensor_copy(out=rwb[0:1, :, :], in_=bsm[0:1, :].rearrange("p (m b) -> p b m", b=2))
 
         nc.vector.quantize_mx(out=wc[:].bitcast(FP8X4), scales=ws[:],
                               in_=wg[:].rearrange("p b m t -> p (b m t)"))
 
-        rwb = const.tile([P, 2, P], F32, name="rwb")
-        nc.vector.tensor_copy(out=rwb[:], in_=bst[:].rearrange("p (m b) -> p b m", b=2))
         pt2 = ps_o.tile([P, 512], F32, name="pt2", tag="ot1")
         bab = const.tile([P, 2], F32, name="bab")
         tmp2 = const.tile([P, NPOS], F32, name="tmp2")
         tmp3 = const.tile([P, NPOS], F32, name="tmp3")
 
-        def bias_transposes():
-            for v in range(2):
-                nc.tensor.transpose(pt2[:, v * P : (v + 1) * P], rwb[:, v, :], ident[:])
+        for v in range(2):
+            nc.tensor.transpose(pt2[:, v * P : (v + 1) * P], rwb[:, v, :], ident[:])
 
         def bias_tables():
             nc.vector.tensor_copy(out=bab[:], in_=pt2[:].rearrange("p (v n) -> p v n", n=P)[:, 0:2, 0])
@@ -235,9 +235,9 @@ def tile_attention_pa_t_kernel(tc, x, Wq, bq, Wk, bk, out_0, out_1):
             for j, s in enumerate(positions(n)):
                 pp = st["pp", s]
                 tt = work.tile([P, 512], F32, name="tt", tag="tt%d" % j)
-                nc.scalar.activation(out=tt[:, 256:512], in_=pp[:, 256:512], func=ACT.Identity,
-                                     bias=bias_b[:, s : s + 1], scale=cos_t[:, s : s + 1])
-                nc.scalar.activation(out=tt[:, 0:256], in_=pp[:, 0:256], func=ACT.Identity,
+                nc.scalar.activation(out=tt[:, 0:256], in_=pp[:, 256:512], func=ACT.Identity,
+                                     bias=bias_b[:, s : s + 1], scale=ncos_t[:, s : s + 1])
+                nc.scalar.activation(out=tt[:, 256:512], in_=pp[:, 0:256], func=ACT.Identity,
                                      bias=bias_a[:, s : s + 1], scale=cos_t[:, s : s + 1])
                 st["tt", s] = tt
 
@@ -246,10 +246,8 @@ def tile_attention_pa_t_kernel(tc, x, Wq, bq, Wk, bk, out_0, out_1):
                 pp = st["pp", s]
                 tt = st["tt", s]
                 oo = work.tile([P, 512], F32, name="oo", tag="oo%d" % j)
-                nc.vector.scalar_tensor_tensor(out=oo[:, 0:256], in0=pp[:, 256:512], scalar=nsin_t[:, s : s + 1],
-                                               in1=tt[:, 0:256], op0=ALU.mult, op1=ALU.add)
-                nc.vector.scalar_tensor_tensor(out=oo[:, 256:512], in0=pp[:, 0:256], scalar=sin_t[:, s : s + 1],
-                                               in1=tt[:, 256:512], op0=ALU.mult, op1=ALU.add)
+                nc.vector.scalar_tensor_tensor(out=oo[:], in0=pp[:], scalar=sin_t[:, s : s + 1],
+                                               in1=tt[:], op0=ALU.mult, op1=ALU.add)
                 st["oo", s] = oo
 
         def stage_t(n):
@@ -257,7 +255,8 @@ def tile_attention_pa_t_kernel(tc, x, Wq, bq, Wk, bk, out_0, out_1):
                 oo = st["oo", s]
                 ot = ps_o.tile([P, 512], F32, name="ot", tag="ot%d" % j)
                 for g in range(4):
-                    nc.tensor.transpose(ot[:, g * P : (g + 1) * P], oo[:, g * P : (g + 1) * P], ident[:])
+                    d = (g + 2) % 4
+                    nc.tensor.transpose(ot[:, d * P : (d + 1) * P], oo[:, g * P : (g + 1) * P], ident[:])
                 st["ot", s] = ot
 
         def stage_c(n):
@@ -265,18 +264,17 @@ def tile_attention_pa_t_kernel(tc, x, Wq, bq, Wk, bk, out_0, out_1):
                 c, i = o_of[s]
                 ln = O_CHUNKS[c]
                 if i == 0:
-                    st["ob", c] = [opool.tile([P, 2 * 8 * NF], F32, name="ob%d" % q) for q in range(2)]
-                src = st["ot", s][:].rearrange("p (b h q m) -> p q h m b", b=2, h=2, q=2)
-                for q in range(2):
-                    dst = st["ob", c][q][:, 0 : 2 * ln * NF].rearrange("p (h s m b) -> p h s m b", h=2, s=ln, b=2)
-                    nc.scalar.copy(out=dst[:, :, i, :, :], in_=src[:, q])
+                    ob = opool.tile([P, 4 * 8 * NF], F32, name="ob")
+                    st["ob", c] = ob
+                ob = st["ob", c]
+                src = st["ot", s][:].rearrange("p (b g m) -> p g m b", b=2, g=4)
+                dst = ob[:, 0 : 4 * ln * NF].rearrange("p (g s m b) -> p g s m b", g=4, s=ln, b=2)
+                nc.scalar.copy(out=dst[:, :, i, :, :], in_=src)
                 if i == ln - 1:
                     first = s - i
+                    obv = ob[:, 0 : 4 * ln * NF].rearrange("p (h q s f) -> p h q s f", h=2, q=2, s=ln)
                     for q in range(2):
-                        nc.sync.dma_start(
-                            out=ov[q][:, :, first : first + ln, :],
-                            in_=st["ob", c][q][:, 0 : 2 * ln * NF].rearrange("p (h s f) -> p h s f", h=2, s=ln),
-                        )
+                        nc.sync.dma_start(out=ov[q][:, :, first : first + ln, :], in_=obv[:, :, q, :, :])
 
         def run(stage, n):
             if 0 <= n < nslot:
@@ -284,8 +282,6 @@ def tile_attention_pa_t_kernel(tc, x, Wq, bq, Wk, bk, out_0, out_1):
 
         for t in range(-1, nslot + 2):
             run(stage_l, t + 1)
-            if t == -1:
-                bias_transposes()
             run(stage_q, t)
             if t == 0:
                 bias_tables()

@@ -25,7 +25,6 @@ FLOPS = 2 * IMAGES * NPOS * E * 2 * NF
 
 X_CHUNKS = [2, 4, 6, 8, 8, 8, 8, 5]
 O_CHUNKS = [8, 8, 8, 8, 8, 4, 2, 2, 1]
-SCALAR_EVAC_EVERY = 4
 
 
 def cos_sin(theta):
@@ -203,7 +202,7 @@ def tile_attention_pa_t_kernel(tc, x, Wq, bq, Wk, bk, out_0, out_1):
             for j, s in enumerate(pos):
                 dst = xg[:, j * 1024 : (j + 1) * 1024].bitcast(F32).rearrange("p (h i u) -> p h i u", h=2, u=2)
                 src = st["xt", s][:].rearrange("p (h u i) -> p h i u", h=2, u=2)
-                if s % SCALAR_EVAC_EVERY == 1:
+                if j == 1:
                     nc.scalar.copy(out=dst, in_=src)
                 else:
                     nc.vector.tensor_copy(out=dst, in_=src)
@@ -237,8 +236,9 @@ def tile_attention_pa_t_kernel(tc, x, Wq, bq, Wk, bk, out_0, out_1):
                 tt = work.tile([P, 512], F32, name="tt", tag="tt%d" % j)
                 nc.scalar.activation(out=tt[:, 0:256], in_=pp[:, 256:512], func=ACT.Identity,
                                      bias=bias_b[:, s : s + 1], scale=ncos_t[:, s : s + 1])
-                nc.scalar.activation(out=tt[:, 256:512], in_=pp[:, 0:256], func=ACT.Identity,
-                                     bias=bias_a[:, s : s + 1], scale=cos_t[:, s : s + 1])
+                if j == 0:
+                    nc.scalar.activation(out=tt[:, 256:512], in_=pp[:, 0:256], func=ACT.Identity,
+                                         bias=bias_a[:, s : s + 1], scale=cos_t[:, s : s + 1])
                 st["tt", s] = tt
 
         def stage_b(n):
@@ -246,8 +246,17 @@ def tile_attention_pa_t_kernel(tc, x, Wq, bq, Wk, bk, out_0, out_1):
                 pp = st["pp", s]
                 tt = st["tt", s]
                 oo = work.tile([P, 512], F32, name="oo", tag="oo%d" % j)
-                nc.vector.scalar_tensor_tensor(out=oo[:], in0=pp[:], scalar=sin_t[:, s : s + 1],
-                                               in1=tt[:], op0=ALU.mult, op1=ALU.add)
+                if j == 0:
+                    nc.vector.scalar_tensor_tensor(out=oo[:], in0=pp[:], scalar=sin_t[:, s : s + 1],
+                                                   in1=tt[:], op0=ALU.mult, op1=ALU.add)
+                else:
+                    nc.vector.scalar_tensor_tensor(out=oo[:, 0:256], in0=pp[:, 0:256], scalar=sin_t[:, s : s + 1],
+                                                   in1=tt[:, 0:256], op0=ALU.mult, op1=ALU.add)
+                    nc.vector.tensor_scalar(out=tt[:, 256:512], in0=pp[:, 0:256], scalar1=cos_t[:, s : s + 1],
+                                            scalar2=bias_a[:, s : s + 1], op0=ALU.mult, op1=ALU.add)
+                    nc.vector.scalar_tensor_tensor(out=oo[:, 256:512], in0=pp[:, 256:512],
+                                                   scalar=sin_t[:, s : s + 1], in1=tt[:, 256:512],
+                                                   op0=ALU.mult, op1=ALU.add)
                 st["oo", s] = oo
 
         def stage_t(n):

@@ -25,6 +25,7 @@ FLOPS = 2 * IMAGES * NPOS * E * 2 * NF
 
 X_CHUNKS = [2, 4, 6, 8, 8, 8, 8, 5]
 O_CHUNKS = [8, 8, 8, 8, 8, 4, 2, 2, 1]
+SCALAR_EVAC_EVERY = 4
 
 
 def cos_sin(theta):
@@ -202,7 +203,7 @@ def tile_attention_pa_t_kernel(tc, x, Wq, bq, Wk, bk, out_0, out_1):
             for j, s in enumerate(pos):
                 dst = xg[:, j * 1024 : (j + 1) * 1024].bitcast(F32).rearrange("p (h i u) -> p h i u", h=2, u=2)
                 src = st["xt", s][:].rearrange("p (h u i) -> p h i u", h=2, u=2)
-                if j == 1:
+                if s % SCALAR_EVAC_EVERY == 1:
                     nc.scalar.copy(out=dst, in_=src)
                 else:
                     nc.vector.tensor_copy(out=dst, in_=src)
@@ -218,6 +219,9 @@ def tile_attention_pa_t_kernel(tc, x, Wq, bq, Wk, bk, out_0, out_1):
             xc, xsc = st["xc", n]
             for j, s in enumerate(positions(n)):
                 pp = ps_p.tile([P, 512], F32, name="pp", tag="pp%d" % j)
+                if j == 0 and len(positions(n)) == 2:
+                    nc.tensor.matmul_mx(out=pp[:], lhsT=wc[:, 0:P].bitcast(FP8X4), lhsT_scale=ws[:, 0:P],
+                                        rhs=xc[:].bitcast(FP8X4), rhs_scale=xsc[:], start=True, stop=True)
                 for ab in range(2):
                     nc.tensor.matmul_mx(
                         out=pp[:, ab * 256 : (ab + 1) * 256],
@@ -236,9 +240,8 @@ def tile_attention_pa_t_kernel(tc, x, Wq, bq, Wk, bk, out_0, out_1):
                 tt = work.tile([P, 512], F32, name="tt", tag="tt%d" % j)
                 nc.scalar.activation(out=tt[:, 0:256], in_=pp[:, 256:512], func=ACT.Identity,
                                      bias=bias_b[:, s : s + 1], scale=ncos_t[:, s : s + 1])
-                if j == 0:
-                    nc.scalar.activation(out=tt[:, 256:512], in_=pp[:, 0:256], func=ACT.Identity,
-                                         bias=bias_a[:, s : s + 1], scale=cos_t[:, s : s + 1])
+                nc.scalar.activation(out=tt[:, 256:512], in_=pp[:, 0:256], func=ACT.Identity,
+                                     bias=bias_a[:, s : s + 1], scale=cos_t[:, s : s + 1])
                 st["tt", s] = tt
 
         def stage_b(n):
@@ -246,17 +249,8 @@ def tile_attention_pa_t_kernel(tc, x, Wq, bq, Wk, bk, out_0, out_1):
                 pp = st["pp", s]
                 tt = st["tt", s]
                 oo = work.tile([P, 512], F32, name="oo", tag="oo%d" % j)
-                if j == 0:
-                    nc.vector.scalar_tensor_tensor(out=oo[:], in0=pp[:], scalar=sin_t[:, s : s + 1],
-                                                   in1=tt[:], op0=ALU.mult, op1=ALU.add)
-                else:
-                    nc.vector.scalar_tensor_tensor(out=oo[:, 0:256], in0=pp[:, 0:256], scalar=sin_t[:, s : s + 1],
-                                                   in1=tt[:, 0:256], op0=ALU.mult, op1=ALU.add)
-                    nc.vector.tensor_scalar(out=tt[:, 256:512], in0=pp[:, 0:256], scalar1=cos_t[:, s : s + 1],
-                                            scalar2=bias_a[:, s : s + 1], op0=ALU.mult, op1=ALU.add)
-                    nc.vector.scalar_tensor_tensor(out=oo[:, 256:512], in0=pp[:, 256:512],
-                                                   scalar=sin_t[:, s : s + 1], in1=tt[:, 256:512],
-                                                   op0=ALU.mult, op1=ALU.add)
+                nc.vector.scalar_tensor_tensor(out=oo[:], in0=pp[:], scalar=sin_t[:, s : s + 1],
+                                               in1=tt[:], op0=ALU.mult, op1=ALU.add)
                 st["oo", s] = oo
 
         def stage_t(n):

from contextlib import ExitStack

import concourse.bass as bass
import concourse.mybir as mybir
import concourse.tile as tile
from concourse.masks import make_identity

F32 = mybir.dt.float32
BF16 = mybir.dt.bfloat16
U32 = mybir.dt.uint32
U8 = mybir.dt.uint8
FP8X4 = mybir.dt.float8_e4m3fn_x4
ALU = mybir.AluOpType
ACT = mybir.ActivationFunctionType

P = 128
IMAGES = 256
GRID = 7
NPOS = GRID * GRID
E = 512
WORDS = E // 2
NF = 128
BASE = 100.0
FLOPS = 2 * IMAGES * NPOS * E * 2 * NF

X_CHUNKS = [2, 4, 6, 8, 8, 8, 8, 5]
O_CHUNKS = [8, 8, 8, 8, 8, 4, 2, 2, 1]
SCALAR_EVAC_EVERY = 4


def cos_sin(theta):
    c, s, term = 0.0, 0.0, 1.0
    for n in range(0, 30, 2):
        c += term
        term = term * theta / (n + 1)
        s += term
        term = -term * theta / (n + 2)
    return c, s


def chunk_table(lens):
    table = []
    for c, n in enumerate(lens):
        for i in range(n):
            table.append((c, i))
    return table


def tile_attention_pa_t_kernel(tc, x, Wq, bq, Wk, bk, out_0, out_1):
    nc = tc.nc
    assert sum(X_CHUNKS) == NPOS and sum(O_CHUNKS) == NPOS
    x_of = chunk_table(X_CHUNKS)
    o_of = chunk_table(O_CHUNKS)
    xv = x.rearrange("(p h) s k -> p h s k", h=2)
    ov = [o.rearrange("(p h) s a d -> p h s (a d)", h=2) for o in (out_0, out_1)]
    nslot = (NPOS + 1) // 2

    with ExitStack() as ctx:
        ctx.enter_context(tc.manual_schedule())
        const = ctx.enter_context(tc.tile_pool(name="const", bufs=1))
        xpool = ctx.enter_context(tc.tile_pool(name="xpool", bufs=1))
        work = ctx.enter_context(tc.tile_pool(name="work", bufs=2))
        opool = ctx.enter_context(tc.tile_pool(name="opool", bufs=3))
        ps_x = ctx.enter_context(tc.psum_pool(name="ps_x", bufs=1))
        ps_p = ctx.enter_context(tc.psum_pool(name="ps_p", bufs=2))
        ps_o = ctx.enter_context(tc.psum_pool(name="ps_o", bufs=1))

        bsm = const.tile([P, 2 * NF], BF16, name="bsm")
        nc.scalar.dma_start(out=bsm[0:1, 0:NF], in_=bq.unsqueeze(0))
        nc.scalar.dma_start(out=bsm[0:1, NF : 2 * NF], in_=bk.unsqueeze(0))
        wraw = const.tile([P, 2, 4, NF], BF16, name="wraw")
        for q, w in enumerate((Wq, Wk)):
            nc.scalar.dma_start(
                out=wraw[:, q, :, :].rearrange("p (u e) f -> p u (e f)", u=2),
                in_=w.rearrange("(u p e) f -> p u (e f)", u=2, e=2),
            )
        xs = []
        s0 = 0
        for c, n in enumerate(X_CHUNKS):
            xt_sb = xpool.tile([P, 2 * n * E], BF16, name="xs%d" % c)
            nc.sync.dma_start(
                out=xt_sb[:].rearrange("p (h s k) -> p h s k", h=2, s=n),
                in_=xv[:, :, s0 : s0 + n, :],
            )
            xs.append(xt_sb)
            s0 += n

        ident = const.tile([P, P], F32, name="ident")
        make_identity(nc, ident[:])
        warm = const.tile([P, 2], F32, name="warm")
        nc.gpsimd.memset(warm[:, 0:1], 0.0)
        nc.scalar.activation(out=warm[:, 1:2], in_=warm[:, 0:1], func=ACT.Identity)

        rw = const.tile([P, 3, P], F32, name="rw")
        nc.vector.memset(rw[:], 0.0)
        rwb = const.tile([P, 2, P], F32, name="rwb")
        nc.vector.memset(rwb[:], 0.0)
        for j in range(8):
            theta = BASE ** (-(2.0 * j) / 16.0)
            for v, val in enumerate(cos_sin(theta)):
                col = rw[:, v, :].rearrange("p (g j) -> p g j", j=8)[:, :, j]
                nc.vector.tensor_scalar(out=col, in0=col, scalar1=val, scalar2=None, op0=ALU.add)
        nc.vector.memset(rw[:, 2, :].rearrange("p (g h j) -> p g h j", h=2, j=8)[:, :, 1, :], 1.0)

        pt = ps_o.tile([P, 512], F32, name="pt", tag="ot0")
        for v in range(3):
            nc.tensor.transpose(pt[:, v * P : (v + 1) * P], rw[:, v, :], ident[:])

        wg = const.tile([P, 2, P, 4], BF16, name="wg", align_bytes=64)
        for ab in range(2):
            nc.scalar.mul(
                out=wg[:, ab, :, :].rearrange("p (q r) t -> p q r t", q=2),
                in_=wraw[:].rearrange("p q t (r b) -> p b q r t", b=2)[:, ab],
                mul=(1.0, -1.0)[ab],
            )
        wc = const.tile([P, 2 * P], U32, name="wc", align_bytes=64)
        ws = const.tile([P, 2 * P], U8, name="ws", align_bytes=64)

        tcs = const.tile([P, 2, GRID], F32, name="tcs")
        h01 = const.tile([P, 2], F32, name="h01")
        nc.vector.memset(tcs[:, 0, 0:1], 1.0)
        nc.vector.memset(tcs[:, 1, 0:1], 0.0)
        ptv = pt[:].rearrange("p (v n) -> p v n", n=P)
        nc.vector.tensor_copy(out=tcs[:, :, 1], in_=ptv[:, 0:2, 0])
        nc.vector.tensor_copy(out=h01[:, 1:2], in_=ptv[:, 2, 0:1])
        nc.vector.tensor_scalar(out=h01[:, 0:1], in0=h01[:, 1:2], scalar1=-1.0, scalar2=1.0,
                                op0=ALU.mult, op1=ALU.add)

        def add_angle(k, lo, hi):
            ck = tcs[:, 0, k : k + 1]
            sk = tcs[:, 1, k : k + 1]
            n = hi - lo
            u = const.tile([P, 2, 2], F32, name="u%d" % k)
            nc.vector.tensor_scalar(out=u[:, :, 0:n], in0=tcs[:, :, lo:hi], scalar1=sk, scalar2=None,
                                    op0=ALU.mult)
            nc.vector.scalar_tensor_tensor(out=tcs[:, 0, lo + k : hi + k], in0=tcs[:, 0, lo:hi], scalar=ck,
                                           in1=u[:, 1, 0:n], op0=ALU.mult, op1=ALU.subtract)
            nc.vector.scalar_tensor_tensor(out=tcs[:, 1, lo + k : hi + k], in0=tcs[:, 1, lo:hi], scalar=ck,
                                           in1=u[:, 0, 0:n], op0=ALU.mult, op1=ALU.add)

        add_angle(1, 1, 2)
        add_angle(2, 1, 3)
        add_angle(4, 1, 3)

        cos_t = const.tile([P, NPOS], F32, name="cos_t")
        sin_t = const.tile([P, NPOS], F32, name="sin_t")
        ncos_t = const.tile([P, NPOS], F32, name="ncos_t")
        bias_a = const.tile([P, NPOS], F32, name="bias_a")
        bias_b = const.tile([P, NPOS], F32, name="bias_b")
        tmp0 = const.tile([P, NPOS], F32, name="tmp0")
        tmp1 = const.tile([P, NPOS], F32, name="tmp1")
        for v, (dst, tmp) in enumerate(((cos_t, tmp0), (sin_t, tmp1))):
            by_col = tcs[:, v, :].unsqueeze(1).to_broadcast([P, GRID, GRID])
            by_row = tcs[:, v, :].unsqueeze(2).to_broadcast([P, GRID, GRID])
            tv = tmp[:].rearrange("p (r c) -> p r c", c=GRID)
            nc.vector.tensor_scalar(out=tv, in0=by_col, scalar1=h01[:, 1:2], scalar2=None, op0=ALU.mult)
            nc.vector.scalar_tensor_tensor(out=dst[:].rearrange("p (r c) -> p r c", c=GRID), in0=by_row,
                                           scalar=h01[:, 0:1], in1=tv, op0=ALU.mult, op1=ALU.add)
        nc.vector.tensor_scalar(out=ncos_t[:], in0=cos_t[:], scalar1=-1.0, scalar2=None, op0=ALU.mult)
        nc.vector.tensor_copy(out=rwb[0:1, :, :], in_=bsm[0:1, :].rearrange("p (m b) -> p b m", b=2))

        nc.vector.quantize_mx(out=wc[:].bitcast(FP8X4), scales=ws[:],
                              in_=wg[:].rearrange("p b m t -> p (b m t)"))

        pt2 = ps_o.tile([P, 512], F32, name="pt2", tag="ot1")
        bab = const.tile([P, 2], F32, name="bab")
        tmp2 = const.tile([P, NPOS], F32, name="tmp2")
        tmp3 = const.tile([P, NPOS], F32, name="tmp3")

        for v in range(2):
            nc.tensor.transpose(pt2[:, v * P : (v + 1) * P], rwb[:, v, :], ident[:])

        def bias_tables():
            nc.vector.tensor_copy(out=bab[:], in_=pt2[:].rearrange("p (v n) -> p v n", n=P)[:, 0:2, 0])
            nc.vector.tensor_scalar(out=tmp2[:], in0=sin_t[:], scalar1=bab[:, 1:2], scalar2=None, op0=ALU.mult)
            nc.vector.scalar_tensor_tensor(out=bias_a[:], in0=cos_t[:], scalar=bab[:, 0:1], in1=tmp2[:],
                                           op0=ALU.mult, op1=ALU.subtract)
            nc.vector.tensor_scalar(out=tmp3[:], in0=cos_t[:], scalar1=bab[:, 1:2], scalar2=None, op0=ALU.mult)
            nc.vector.scalar_tensor_tensor(out=bias_b[:], in0=sin_t[:], scalar=bab[:, 0:1], in1=tmp3[:],
                                           op0=ALU.mult, op1=ALU.add)

        st = {}

        def positions(n):
            return [s for s in (2 * n, 2 * n + 1) if s < NPOS]

        def stage_l(n):
            for j, s in enumerate(positions(n)):
                c, i = x_of[s]
                x32 = xs[c][:].bitcast(F32)
                xt = ps_x.tile([P, 512], F32, name="xt", tag="xt%d" % j)
                for h in range(2):
                    for u in range(2):
                        off = (h * X_CHUNKS[c] + i) * WORDS + u * P
                        nc.tensor.transpose(xt[:, (2 * h + u) * P : (2 * h + u + 1) * P],
                                            x32[:, off : off + P], ident[:])
                st["xt", s] = xt

        def stage_e(n):
            pos = positions(n)
            xg = work.tile([P, 2048], BF16, name="xg", align_bytes=64)
            st["xg", n] = xg
            for j, s in enumerate(pos):
                dst = xg[:, j * 1024 : (j + 1) * 1024].bitcast(F32).rearrange("p (h i u) -> p h i u", h=2, u=2)
                src = st["xt", s][:].rearrange("p (h u i) -> p h i u", h=2, u=2)
                if s % SCALAR_EVAC_EVERY == 1:
                    nc.scalar.copy(out=dst, in_=src)
                else:
                    nc.vector.tensor_copy(out=dst, in_=src)

        def stage_q(n):
            w = 256 * len(positions(n))
            xc = work.tile([P, 512], U32, name="xc", align_bytes=64)
            xsc = work.tile([P, 512], U8, name="xsc", align_bytes=64)
            nc.vector.quantize_mx(out=xc[:, 0:w].bitcast(FP8X4), scales=xsc[:, 0:w], in_=st["xg", n][:, 0 : 4 * w])
            st["xc", n] = (xc, xsc)

        def stage_m(n):
            xc, xsc = st["xc", n]
            for j, s in enumerate(positions(n)):
                pp = ps_p.tile([P, 512], F32, name="pp", tag="pp%d" % j)
                if j == 0 and len(positions(n)) == 2:
                    nc.tensor.matmul_mx(out=pp[:], lhsT=wc[:, 0:P].bitcast(FP8X4), lhsT_scale=ws[:, 0:P],
                                        rhs=xc[:].bitcast(FP8X4), rhs_scale=xsc[:], start=True, stop=True)
                for ab in range(2):
                    nc.tensor.matmul_mx(
                        out=pp[:, ab * 256 : (ab + 1) * 256],
                        lhsT=wc[:, ab * P : (ab + 1) * P].bitcast(FP8X4),
                        lhsT_scale=ws[:, ab * P : (ab + 1) * P],
                        rhs=xc[:, j * 256 : (j + 1) * 256].bitcast(FP8X4),
                        rhs_scale=xsc[:, j * 256 : (j + 1) * 256],
                        start=True,
                        stop=True,
                    )
                st["pp", s] = pp

        def stage_a(n):
            for j, s in enumerate(positions(n)):
                pp = st["pp", s]
                tt = work.tile([P, 512], F32, name="tt", tag="tt%d" % j)
                nc.scalar.activation(out=tt[:, 0:256], in_=pp[:, 256:512], func=ACT.Identity,
                                     bias=bias_b[:, s : s + 1], scale=ncos_t[:, s : s + 1])
                nc.scalar.activation(out=tt[:, 256:512], in_=pp[:, 0:256], func=ACT.Identity,
                                     bias=bias_a[:, s : s + 1], scale=cos_t[:, s : s + 1])
                st["tt", s] = tt

        def stage_b(n):
            for j, s in enumerate(positions(n)):
                pp = st["pp", s]
                tt = st["tt", s]
                oo = work.tile([P, 512], F32, name="oo", tag="oo%d" % j)
                nc.vector.scalar_tensor_tensor(out=oo[:], in0=pp[:], scalar=sin_t[:, s : s + 1],
                                               in1=tt[:], op0=ALU.mult, op1=ALU.add)
                st["oo", s] = oo

        def stage_t(n):
            for j, s in enumerate(positions(n)):
                oo = st["oo", s]
                ot = ps_o.tile([P, 512], F32, name="ot", tag="ot%d" % j)
                for g in range(4):
                    d = (g + 2) % 4
                    nc.tensor.transpose(ot[:, d * P : (d + 1) * P], oo[:, g * P : (g + 1) * P], ident[:])
                st["ot", s] = ot

        def stage_c(n):
            for s in positions(n):
                c, i = o_of[s]
                ln = O_CHUNKS[c]
                if i == 0:
                    ob = opool.tile([P, 4 * 8 * NF], F32, name="ob")
                    st["ob", c] = ob
                ob = st["ob", c]
                src = st["ot", s][:].rearrange("p (b g m) -> p g m b", b=2, g=4)
                dst = ob[:, 0 : 4 * ln * NF].rearrange("p (g s m b) -> p g s m b", g=4, s=ln, b=2)
                nc.scalar.copy(out=dst[:, :, i, :, :], in_=src)
                if i == ln - 1:
                    first = s - i
                    obv = ob[:, 0 : 4 * ln * NF].rearrange("p (h q s f) -> p h q s f", h=2, q=2, s=ln)
                    for q in range(2):
                        nc.sync.dma_start(out=ov[q][:, :, first : first + ln, :], in_=obv[:, :, q, :, :])

        def run(stage, n):
            if 0 <= n < nslot:
                stage(n)

        for t in range(-1, nslot + 2):
            run(stage_l, t + 1)
            run(stage_q, t)
            if t == 0:
                bias_tables()
            run(stage_a, t - 1)
            run(stage_e, t + 1)
            run(stage_t, t - 2)
            run(stage_b, t - 1)
            run(stage_c, t - 2)
            run(stage_m, t)
